import numpy as np
import ml_dtypes


def mxq(x, axis, fmt="e4m3"):
    dtype, down = {"e4m3": (ml_dtypes.float8_e4m3fn, 7), "e5m2": (ml_dtypes.float8_e5m2, 14)}[fmt]
    v = np.moveaxis(np.asarray(x, np.float32).astype(ml_dtypes.bfloat16).astype(np.float64), axis, -1)
    blocks = v.reshape(v.shape[:-1] + (-1, 32))
    amax = np.abs(blocks).max(-1, keepdims=True)
    byte = np.maximum(np.where(amax > 0, np.frexp(amax)[1] - 1 + 127, 0) - down, 1)
    scale = np.exp2(byte - 127.0)
    codes = (blocks / scale).astype(np.float32).astype(dtype).astype(np.float64)
    return np.moveaxis((codes * scale).reshape(v.shape), -1, axis)


WIDE = False


def mx_kscale(k):
    if not WIDE:
        return np.ones(k)
    levels = np.array([10, -10, 5, -5, 0])
    a = np.random.permutation(np.resize(levels, k // 512 * 4)).reshape(k // 512, 4)
    idx = np.arange(k)
    return np.exp2(a[idx // 512, idx % 128 // 32])


BF16 = ml_dtypes.bfloat16


def bf(x):
    return np.asarray(x, np.float32).astype(BF16)


def f64(x):
    return np.asarray(x).astype(np.float64)


B, C, C4, H, W, R = 1, 512, 512, 64, 64, 4
ND = 2 * R + 1
GAIN = 1.2
QS = GAIN * C4 ** 0.25
BS = 0.3 * QS


def setup_inputs():
    s, t = mx_kscale(C), mx_kscale(C4)
    return {"x": bf(np.random.standard_normal((B, C, H, W)) * s[None, :, None, None]),
            "y": bf(np.random.standard_normal((B, C, H, W)) * s[None, :, None, None]),
            "query_w": bf(np.random.standard_normal((C4, C)) * QS / np.sqrt(C) * t[:, None] / s[None, :]),
            "query_b": bf(np.random.standard_normal(C4) * BS * t),
            "key_w": bf(np.random.standard_normal((C4, C)) * QS / np.sqrt(C) / t[:, None] / s[None, :]),
            "key_b": bf(np.random.standard_normal(C4) * BS / t)}


def reference(x, y, query_w, query_b, key_w, key_b):
    yq = mxq(f64(y).reshape(B, C, H * W), 1, "e4m3")
    xq = mxq(f64(x).reshape(B, C, H * W), 1, "e4m3")
    q = (mxq(f64(query_w), 1, "e4m3") @ yq) + f64(query_b)[None, :, None]
    k = (mxq(f64(key_w), 1, "e4m3") @ xq) + f64(key_b)[None, :, None]
    qq = mxq(q, 1, "e4m3").reshape(B, C4, H, W).transpose(0, 2, 3, 1)
    kq = mxq(k, 1, "e4m3").reshape(B, C4, H, W).transpose(0, 2, 1, 3)
    corr = np.zeros((B, H, W, ND * ND))
    for di in range(ND):
        oi = di - R
        i0, i1 = max(0, -oi), min(H, H - oi)
        sc = qq[:, i0:i1] @ kq[:, i0 + oi:i1 + oi]
        for dj in range(ND):
            oj = dj - R
            w0, w1 = max(0, -oj), min(W, W - oj)
            corr[:, i0:i1, w0:w1, di * ND + dj] = np.diagonal(sc, offset=oj, axis1=2, axis2=3)
    corr = corr / C4
    e = np.exp(corr - corr.max(-1, keepdims=True))
    return e / e.sum(-1, keepdims=True)

@@ -1,0 +1,288 @@
+from contextlib import ExitStack
+
+import concourse.mybir as mybir
+from concourse.masks import make_identity
+
+F32 = mybir.dt.float32
+BF16 = mybir.dt.bfloat16
+U32 = mybir.dt.uint32
+U8 = mybir.dt.uint8
+I32 = mybir.dt.int32
+FP8X4 = mybir.dt.float8_e4m3fn_x4
+
+P = 128
+PACK = 4
+CHANNELS = P * PACK
+HEIGHT = 64
+WIDTH = 64
+REACH = 4
+SHIFTS = 2 * REACH + 1
+CELLS = SHIFTS * SHIFTS
+
+BLOCK_ROWS = 8
+BLOCKS = HEIGHT // BLOCK_ROWS
+BLOCK_PIXELS = BLOCK_ROWS * WIDTH
+PAIR_PIXELS = 2 * WIDTH
+PAIRS = BLOCK_ROWS // 2
+
+PATCH_COLS = P // BLOCK_ROWS
+PATCHES = WIDTH // PATCH_COLS
+WINDOW_ROWS = BLOCK_ROWS + 2 * REACH
+WINDOW_COLS = PATCH_COLS + 2 * REACH
+K_BLOCKS = BLOCKS + 1
+K_MARGIN = 8
+K_COLS = WIDTH + 2 * K_MARGIN
+K_BLOCK_WORDS = K_COLS * BLOCK_ROWS
+STREAM_COLS = 32
+STREAM_SKIP = K_MARGIN - REACH
+
+PARK_RUN = SHIFTS * WINDOW_COLS
+PARK_STEP = PARK_RUN + 1
+PARK_READ = (SHIFTS - 1) * WINDOW_COLS + SHIFTS
+PARK_ROW = WIDTH * PARK_STEP
+PARK_BLOCK = BLOCK_ROWS * PARK_ROW
+PARK_SLOTS = 2
+OUT_FLOATS = HEIGHT * WIDTH * CELLS
+OUT_BLOCK = BLOCK_PIXELS * CELLS
+PARK_START = OUT_FLOATS - PARK_SLOTS * PARK_BLOCK
+
+FLOPS = 2 * 2 * CHANNELS * CHANNELS * HEIGHT * WIDTH + 2 * CHANNELS * CELLS * HEIGHT * WIDTH
+
+
+def park_base(block):
+    return PARK_START + (block % PARK_SLOTS) * PARK_BLOCK
+
+
+def last_block_parked_on(block):
+    first, end = block * OUT_BLOCK, (block + 1) * OUT_BLOCK
+    users = [b for b in range(BLOCKS) if park_base(b) < end and first < park_base(b) + PARK_BLOCK]
+    return max(users) if users else -1
+
+
+def tile_local_module_pa_t_kernel(tc, x, y, query_w, query_b, key_w, key_b, out):
+    nc = tc.nc
+    with ExitStack() as ctx:
+        keep = ctx.enter_context(tc.tile_pool(name="keep", bufs=1))
+        weight_stage = ctx.enter_context(tc.tile_pool(name="weight_stage", bufs=2))
+        raw_pool = ctx.enter_context(tc.tile_pool(name="raw", bufs=3))
+        stage = ctx.enter_context(tc.tile_pool(name="stage", bufs=2))
+        k_stage = ctx.enter_context(tc.tile_pool(name="k_stage", bufs=3))
+        small = ctx.enter_context(tc.tile_pool(name="small", bufs=2))
+        flip_psum = ctx.enter_context(tc.psum_pool(name="flip_psum", bufs=1))
+        project_psum = ctx.enter_context(tc.psum_pool(name="project_psum", bufs=4))
+        corr_psum = ctx.enter_context(tc.psum_pool(name="corr_psum", bufs=3))
+
+        q_codes = keep.tile([P, BLOCKS * BLOCK_PIXELS], U32, align_bytes=64)
+        q_scales = keep.tile([P, BLOCKS * BLOCK_PIXELS], U8, align_bytes=64)
+        k_codes = keep.tile([P, K_BLOCKS * K_BLOCK_WORDS], U32, align_bytes=64)
+        k_scales = keep.tile([P, K_BLOCKS * K_BLOCK_WORDS], U8, align_bytes=64)
+        result = keep.tile([P, BLOCKS, PAIRS, CELLS], F32)
+        identity = keep.tile([P, P], BF16)
+        make_identity(nc, identity[:])
+
+        margin_words = K_MARGIN * BLOCK_ROWS
+        code_blocks = k_codes[:].bitcast(I32).rearrange("p (b w) -> p b w", w=K_BLOCK_WORDS)
+        scale_blocks = k_scales[:].bitcast(I32).rearrange("p (b w) -> p b w", w=K_BLOCK_WORDS // 4)
+        nc.vector.memset(code_blocks[:, :, 0:margin_words], 0)
+        nc.vector.memset(code_blocks[:, :, K_BLOCK_WORDS - margin_words :], 0)
+        nc.vector.memset(scale_blocks[:, :, 0 : margin_words // 4], 0)
+        nc.vector.memset(scale_blocks[:, :, (K_BLOCK_WORDS - margin_words) // 4 :], 0)
+
+        def quantise_weight(w, name):
+            rows = weight_stage.tile([P, PACK, CHANNELS], BF16, name="w_rows")
+            nc.sync.dma_start(out=rows[:], in_=w.rearrange("(p m) c -> p m c", m=PACK))
+            grouped = weight_stage.tile([P, CHANNELS, PACK], BF16, name="w_grouped", align_bytes=64)
+            for m in range(PACK):
+                flipped = flip_psum.tile([P, PACK, P], BF16, name="flipped")
+                for j in range(PACK):
+                    nc.tensor.transpose(flipped[:, j, :], rows[:, m, j * P : (j + 1) * P], identity[:])
+                nc.vector.tensor_copy(
+                    out=grouped[:, m * P : (m + 1) * P, :], in_=flipped[:].rearrange("p j o -> p o j")
+                )
+            codes = keep.tile([P, CHANNELS], U32, name=name + "_codes", align_bytes=64)
+            scales = keep.tile([P, CHANNELS], U8, name=name + "_scales", align_bytes=64)
+            nc.vector.quantize_mx(
+                out=codes[:].bitcast(FP8X4), scales=scales[:], in_=grouped[:].rearrange("p o j -> p (o j)")
+            )
+            return codes, scales
+
+        def load_bias(b, name):
+            bias = keep.tile([P, PACK], BF16, name=name)
+            nc.sync.dma_start(out=bias[:], in_=b.rearrange("(p t) -> p t", t=PACK))
+            return bias
+
+        key_weight = quantise_weight(key_w, "key_w")
+        query_weight = quantise_weight(query_w, "query_w")
+        key_bias = load_bias(key_b, "key_bias")
+        query_bias = load_bias(query_b, "query_bias")
+
+        def quantise_input(image, block, name):
+            planes = image.rearrange("b (j p) h w -> p (b j) (h w)", p=P)
+            raw = raw_pool.tile([P, PACK, BLOCK_PIXELS], BF16, name=name + "_raw")
+            nc.sync.dma_start(out=raw[:], in_=planes[:, :, block * BLOCK_PIXELS : (block + 1) * BLOCK_PIXELS])
+            grouped = stage.tile([P, BLOCK_PIXELS, PACK], BF16, name=name + "_grouped", align_bytes=64)
+            nc.scalar.copy(
+                out=grouped[:].rearrange("p (c i) j -> p c j i", i=4),
+                in_=raw[:].rearrange("p j (c i) -> p c j i", i=4),
+            )
+            codes = stage.tile([P, BLOCK_PIXELS], U32, name=name + "_codes", align_bytes=64)
+            scales = stage.tile([P, BLOCK_PIXELS], U8, name=name + "_scales", align_bytes=64)
+            nc.vector.quantize_mx(
+                out=codes[:].bitcast(FP8X4), scales=scales[:], in_=grouped[:].rearrange("p w j -> p (w j)")
+            )
+            return codes, scales
+
+        def project(pixels, pair, weight, bias, target):
+            codes, scales = pixels
+            w_codes, w_scales = weight
+            cols = slice(pair * PAIR_PIXELS, (pair + 1) * PAIR_PIXELS)
+            bank = project_psum.tile([P, PACK, PAIR_PIXELS], F32, name="bank")
+            for t in range(PACK):
+                channels = slice(t * P, (t + 1) * P)
+                nc.tensor.matmul_mx(
+                    out=bank[:, t, :],
+                    lhsT=w_codes[:, channels].bitcast(FP8X4),
+                    lhsT_scale=w_scales[:, channels],
+                    rhs=codes[:, cols].bitcast(FP8X4),
+                    rhs_scale=scales[:, cols],
+                    start=True,
+                    stop=True,
+                )
+            nc.vector.tensor_tensor(
+                out=target,
+                in0=bank[:].rearrange("p t (i j) -> p j i t", i=2),
+                in1=bias[:].unsqueeze(1).unsqueeze(1).to_broadcast([P, WIDTH, 2, PACK]),
+                op=mybir.AluOpType.add,
+            )
+
+        def new_k_block(k_block):
+            grouped = k_stage.tile([P, WIDTH, BLOCK_ROWS, PACK], BF16, name="k_grouped", align_bytes=64)
+            if k_block == 0:
+                nc.vector.memset(grouped[:, :, 0:REACH, :], 0.0)
+            if k_block == K_BLOCKS - 1:
+                nc.vector.memset(grouped[:, :, REACH:, :], 0.0)
+            return grouped
+
+        def quantise_k_block(grouped, k_block):
+            first = k_block * K_BLOCK_WORDS + margin_words
+            nc.vector.quantize_mx(
+                out=k_codes[:, first : first + BLOCK_PIXELS].bitcast(FP8X4),
+                scales=k_scales[:, first : first + BLOCK_PIXELS],
+                in_=grouped[:].rearrange("p j r t -> p (j r t)"),
+            )
+
+        out_flat = out.rearrange("b h w d -> (b h w d)")
+        out_pixels = out.rearrange("b h w d -> (b h w) d")
+
+        def correlate(block):
+            products = stage.tile([P, PATCHES, WINDOW_ROWS * WINDOW_COLS], F32, name="products")
+            for patch in range(PATCHES):
+                q_cols = slice(block * BLOCK_PIXELS + patch * P, block * BLOCK_PIXELS + (patch + 1) * P)
+                bank = corr_psum.tile([P, 2, STREAM_COLS * BLOCK_ROWS], F32, name="corr_bank")
+                for half in range(2):
+                    first = (block + half) * K_BLOCK_WORDS + patch * PATCH_COLS * BLOCK_ROWS
+                    k_cols = slice(first, first + STREAM_COLS * BLOCK_ROWS)
+                    nc.tensor.matmul_mx(
+                        out=bank[:, half, :],
+                        lhsT=q_codes[:, q_cols].bitcast(FP8X4),
+                        lhsT_scale=q_scales[:, q_cols],
+                        rhs=k_codes[:, k_cols].bitcast(FP8X4),
+                        rhs_scale=k_scales[:, k_cols],
+                        start=True,
+                        stop=True,
+                    )
+                nc.scalar.copy(
+                    out=products[:, patch, :].rearrange("p (h r c) -> p h r c", h=2, r=BLOCK_ROWS),
+                    in_=bank[:].rearrange("p h (c r) -> p h r c", r=BLOCK_ROWS)[
+                        :, :, :, STREAM_SKIP : STREAM_SKIP + WINDOW_COLS
+                    ],
+                )
+            for r in range(BLOCK_ROWS):
+                row_base = park_base(block) + r * PARK_ROW
+                parked = (
+                    out_flat[row_base : row_base + PARK_ROW]
+                    .rearrange("(a s) -> a s", s=PATCH_COLS * PARK_STEP)[:, 0 : PATCH_COLS * PARK_RUN]
+                    .rearrange("a (c s) -> c a s", s=PARK_RUN)
+                )
+                nc.sync.dma_start(
+                    out=parked, in_=products[r:P:BLOCK_ROWS, :, r * WINDOW_COLS : r * WINDOW_COLS + PARK_RUN]
+                )
+
+        def softmax(block):
+            windows = stage.tile([P, PAIRS, PARK_RUN], F32, name="windows")
+            base = park_base(block)
+            nc.sync.dma_start(
+                out=windows[:, :, 0:PARK_READ],
+                in_=out_flat[base : base + PARK_BLOCK].rearrange("(m p s) -> p m s", p=P, s=PARK_STEP)[
+                    :, :, 0:PARK_READ
+                ],
+            )
+            corr = windows[:].rearrange("p m (d c) -> p m d c", c=WINDOW_COLS)[:, :, :, 0:SHIFTS]
+            top = small.tile([P, PAIRS], F32, name="top")
+            nc.vector.tensor_reduce(out=top[:], in_=corr, axis=mybir.AxisListType.XY, op=mybir.AluOpType.max)
+            shift = small.tile([P, PAIRS], F32, name="shift")
+            nc.vector.tensor_scalar_mul(out=shift[:], in0=top[:], scalar1=-1.0 / CHANNELS)
+            powers = stage.tile([P, PAIRS, CELLS], F32, name="powers")
+            total = small.tile([P, PAIRS], F32, name="total")
+            for m in range(PAIRS):
+                nc.scalar.activation(
+                    out=powers[:, m, :].rearrange("p (d c) -> p d c", c=SHIFTS),
+                    in_=corr[:, m],
+                    func=mybir.ActivationFunctionType.Exp,
+                    bias=shift[:, m : m + 1],
+                    scale=1.0 / CHANNELS,
+                    accum_out=total[:, m : m + 1],
+                )
+            inverse = small.tile([P, PAIRS], F32, name="inverse")
+            nc.vector.reciprocal(out=inverse[:], in_=total[:])
+            for m in range(PAIRS):
+                nc.gpsimd.tensor_scalar(
+                    out=result[:, block, m, :],
+                    in0=powers[:, m, :],
+                    scalar1=inverse[:, m : m + 1],
+                    scalar2=0.0,
+                    op0=mybir.AluOpType.mult,
+                    op1=mybir.AluOpType.add,
+                )
+
+        def store(block):
+            nc.sync.dma_start(
+                out=out_pixels[block * BLOCK_PIXELS : (block + 1) * BLOCK_PIXELS, :].rearrange(
+                    "(m p) d -> p m d", p=P
+                ),
+                in_=result[:, block],
+            )
+
+        def finish(block):
+            softmax(block)
+            for done in range(block + 1):
+                if max(done, last_block_parked_on(done)) == block:
+                    store(done)
+
+        k_grouped = new_k_block(0)
+        for block in range(BLOCKS):
+            x_pixels = quantise_input(x, block, "x")
+            y_pixels = quantise_input(y, block, "y")
+            for pair in range(PAIRS // 2):
+                rows = slice(REACH + 2 * pair, REACH + 2 * pair + 2)
+                project(x_pixels, pair, key_weight, key_bias, k_grouped[:, :, rows, :])
+            quantise_k_block(k_grouped, block)
+            if block > 0:
+                correlate(block - 1)
+            q_grouped = stage.tile([P, WIDTH, BLOCK_ROWS, PACK], BF16, name="q_grouped", align_bytes=64)
+            for pair in range(PAIRS):
+                project(y_pixels, pair, query_weight, query_bias, q_grouped[:, :, 2 * pair : 2 * pair + 2, :])
+            nc.vector.quantize_mx(
+                out=q_codes[:, block * BLOCK_PIXELS : (block + 1) * BLOCK_PIXELS].bitcast(FP8X4),
+                scales=q_scales[:, block * BLOCK_PIXELS : (block + 1) * BLOCK_PIXELS],
+                in_=q_grouped[:].rearrange("p j r t -> p (j r t)"),
+            )
+            k_grouped = new_k_block(block + 1)
+            for pair in range(PAIRS // 2, PAIRS):
+                rows = slice(2 * pair - REACH, 2 * pair - REACH + 2)
+                project(x_pixels, pair, key_weight, key_bias, k_grouped[:, :, rows, :])
+            if block > 0:
+                finish(block - 1)
+        quantise_k_block(k_grouped, K_BLOCKS - 1)
+        correlate(BLOCKS - 1)
+        finish(BLOCKS - 1)

@@ -68,9 +68,8 @@ def tile_local_module_pa_t_kernel(tc, x, y, query_w, query_b, key_w, key_b, out)
         stage = ctx.enter_context(tc.tile_pool(name="stage", bufs=2))
         k_stage = ctx.enter_context(tc.tile_pool(name="k_stage", bufs=3))
         small = ctx.enter_context(tc.tile_pool(name="small", bufs=2))
-        flip_psum = ctx.enter_context(tc.psum_pool(name="flip_psum", bufs=1))
         project_psum = ctx.enter_context(tc.psum_pool(name="project_psum", bufs=4))
-        corr_psum = ctx.enter_context(tc.psum_pool(name="corr_psum", bufs=3))
+        corr_psum = ctx.enter_context(tc.psum_pool(name="corr_psum", bufs=4))
 
         q_codes = keep.tile([P, BLOCKS * BLOCK_PIXELS], U32, align_bytes=64)
         q_scales = keep.tile([P, BLOCKS * BLOCK_PIXELS], U8, align_bytes=64)
@@ -88,12 +87,15 @@ def tile_local_module_pa_t_kernel(tc, x, y, query_w, query_b, key_w, key_b, out)
         nc.vector.memset(scale_blocks[:, :, 0 : margin_words // 4], 0)
         nc.vector.memset(scale_blocks[:, :, (K_BLOCK_WORDS - margin_words) // 4 :], 0)
 
-        def quantise_weight(w, name):
+        def load_weight(w):
             rows = weight_stage.tile([P, PACK, CHANNELS], BF16, name="w_rows")
             nc.sync.dma_start(out=rows[:], in_=w.rearrange("(p m) c -> p m c", m=PACK))
+            return rows
+
+        def quantise_weight(rows, name):
             grouped = weight_stage.tile([P, CHANNELS, PACK], BF16, name="w_grouped", align_bytes=64)
             for m in range(PACK):
-                flipped = flip_psum.tile([P, PACK, P], BF16, name="flipped")
+                flipped = corr_psum.tile([P, PACK, P], BF16, name="flipped", tag="corr_bank")
                 for j in range(PACK):
                     nc.tensor.transpose(flipped[:, j, :], rows[:, m, j * P : (j + 1) * P], identity[:])
                 nc.vector.tensor_copy(
@@ -111,20 +113,21 @@ def tile_local_module_pa_t_kernel(tc, x, y, query_w, query_b, key_w, key_b, out)
             nc.sync.dma_start(out=bias[:], in_=b.rearrange("(p t) -> p t", t=PACK))
             return bias
 
-        key_weight = quantise_weight(key_w, "key_w")
-        query_weight = quantise_weight(query_w, "query_w")
-        key_bias = load_bias(key_b, "key_bias")
-        query_bias = load_bias(query_b, "query_bias")
-
-        def quantise_input(image, block, name):
+        def load_input(image, block, name):
             planes = image.rearrange("b (j p) h w -> p (b j) (h w)", p=P)
             raw = raw_pool.tile([P, PACK, BLOCK_PIXELS], BF16, name=name + "_raw")
             nc.sync.dma_start(out=raw[:], in_=planes[:, :, block * BLOCK_PIXELS : (block + 1) * BLOCK_PIXELS])
+            return raw
+
+        def regroup_input(raw, name):
             grouped = stage.tile([P, BLOCK_PIXELS, PACK], BF16, name=name + "_grouped", align_bytes=64)
             nc.scalar.copy(
                 out=grouped[:].rearrange("p (c i) j -> p c j i", i=4),
                 in_=raw[:].rearrange("p j (c i) -> p c j i", i=4),
             )
+            return grouped
+
+        def quantise_input(grouped, name):
             codes = stage.tile([P, BLOCK_PIXELS], U32, name=name + "_codes", align_bytes=64)
             scales = stage.tile([P, BLOCK_PIXELS], U8, name=name + "_scales", align_bytes=64)
             nc.vector.quantize_mx(
@@ -208,7 +211,7 @@ def tile_local_module_pa_t_kernel(tc, x, y, query_w, query_b, key_w, key_b, out)
                     out=parked, in_=products[r:P:BLOCK_ROWS, :, r * WINDOW_COLS : r * WINDOW_COLS + PARK_RUN]
                 )
 
-        def softmax(block):
+        def read_back(block):
             windows = stage.tile([P, PAIRS, PARK_RUN], F32, name="windows")
             base = park_base(block)
             nc.sync.dma_start(
@@ -217,33 +220,39 @@ def tile_local_module_pa_t_kernel(tc, x, y, query_w, query_b, key_w, key_b, out)
                     :, :, 0:PARK_READ
                 ],
             )
-            corr = windows[:].rearrange("p m (d c) -> p m d c", c=WINDOW_COLS)[:, :, :, 0:SHIFTS]
+            return windows
+
+        def window_cells(windows):
+            return windows[:].rearrange("p m (d c) -> p m d c", c=WINDOW_COLS)[:, :, :, 0:SHIFTS]
+
+        def softmax_shift(windows):
             top = small.tile([P, PAIRS], F32, name="top")
-            nc.vector.tensor_reduce(out=top[:], in_=corr, axis=mybir.AxisListType.XY, op=mybir.AluOpType.max)
+            nc.vector.tensor_reduce(
+                out=top[:], in_=window_cells(windows), axis=mybir.AxisListType.XY, op=mybir.AluOpType.max
+            )
             shift = small.tile([P, PAIRS], F32, name="shift")
             nc.vector.tensor_scalar_mul(out=shift[:], in0=top[:], scalar1=-1.0 / CHANNELS)
+            return shift
+
+        def softmax_powers(windows, shift):
             powers = stage.tile([P, PAIRS, CELLS], F32, name="powers")
             total = small.tile([P, PAIRS], F32, name="total")
             for m in range(PAIRS):
                 nc.scalar.activation(
                     out=powers[:, m, :].rearrange("p (d c) -> p d c", c=SHIFTS),
-                    in_=corr[:, m],
+                    in_=window_cells(windows)[:, m],
                     func=mybir.ActivationFunctionType.Exp,
                     bias=shift[:, m : m + 1],
                     scale=1.0 / CHANNELS,
                     accum_out=total[:, m : m + 1],
                 )
+            return powers, total
+
+        def softmax_divide(block, powers, total):
             inverse = small.tile([P, PAIRS], F32, name="inverse")
             nc.vector.reciprocal(out=inverse[:], in_=total[:])
             for m in range(PAIRS):
-                nc.gpsimd.tensor_scalar(
-                    out=result[:, block, m, :],
-                    in0=powers[:, m, :],
-                    scalar1=inverse[:, m : m + 1],
-                    scalar2=0.0,
-                    op0=mybir.AluOpType.mult,
-                    op1=mybir.AluOpType.add,
-                )
+                nc.scalar.mul(out=result[:, block, m, :], in_=powers[:, m, :], mul=inverse[:, m : m + 1])
 
         def store(block):
             nc.sync.dma_start(
@@ -253,36 +262,81 @@ def tile_local_module_pa_t_kernel(tc, x, y, query_w, query_b, key_w, key_b, out)
                 in_=result[:, block],
             )
 
-        def finish(block):
-            softmax(block)
+        def store_what_is_free(block):
             for done in range(block + 1):
                 if max(done, last_block_parked_on(done)) == block:
                     store(done)
 
+        def project_k(pixels, pair, grouped):
+            first = (2 * pair + REACH) % BLOCK_ROWS
+            project(pixels, pair, key_weight, key_bias, grouped[:, :, first : first + 2, :])
+
+        def project_q(pixels, pair, grouped):
+            project(pixels, pair, query_weight, query_bias, grouped[:, :, 2 * pair : 2 * pair + 2, :])
+
+        ctx.enter_context(tc.manual_schedule())
+        key_rows = load_weight(key_w)
+        x_raw = {0: load_input(x, 0, "x")}
+        query_rows = load_weight(query_w)
+        y_raw = {0: load_input(y, 0, "y")}
+        key_bias = load_bias(key_b, "key_bias")
+        query_bias = load_bias(query_b, "query_bias")
+        x_raw[1] = load_input(x, 1, "x")
+        y_raw[1] = load_input(y, 1, "y")
+
+        key_weight = quantise_weight(key_rows, "key_w")
+        x_grouped = regroup_input(x_raw[0], "x")
+        y_grouped = regroup_input(y_raw[0], "y")
+        x_pixels = quantise_input(x_grouped, "x")
+        query_weight = quantise_weight(query_rows, "query_w")
+
         k_grouped = new_k_block(0)
-        for block in range(BLOCKS):
-            x_pixels = quantise_input(x, block, "x")
-            y_pixels = quantise_input(y, block, "y")
-            for pair in range(PAIRS // 2):
-                rows = slice(REACH + 2 * pair, REACH + 2 * pair + 2)
-                project(x_pixels, pair, key_weight, key_bias, k_grouped[:, :, rows, :])
-            quantise_k_block(k_grouped, block)
-            if block > 0:
-                correlate(block - 1)
-            q_grouped = stage.tile([P, WIDTH, BLOCK_ROWS, PACK], BF16, name="q_grouped", align_bytes=64)
-            for pair in range(PAIRS):
-                project(y_pixels, pair, query_weight, query_bias, q_grouped[:, :, 2 * pair : 2 * pair + 2, :])
-            nc.vector.quantize_mx(
-                out=q_codes[:, block * BLOCK_PIXELS : (block + 1) * BLOCK_PIXELS].bitcast(FP8X4),
-                scales=q_scales[:, block * BLOCK_PIXELS : (block + 1) * BLOCK_PIXELS],
-                in_=q_grouped[:].rearrange("p j r t -> p (j r t)"),
-            )
-            k_grouped = new_k_block(block + 1)
-            for pair in range(PAIRS // 2, PAIRS):
-                rows = slice(2 * pair - REACH, 2 * pair - REACH + 2)
-                project(x_pixels, pair, key_weight, key_bias, k_grouped[:, :, rows, :])
-            if block > 0:
-                finish(block - 1)
-        quantise_k_block(k_grouped, K_BLOCKS - 1)
-        correlate(BLOCKS - 1)
-        finish(BLOCKS - 1)
+        windows = {}
+        shift = {}
+        for step in range(BLOCKS + 3):
+            projecting = step < BLOCKS
+            preparing = step + 1 < BLOCKS
+            correlating = 0 <= step - 1 < BLOCKS
+            shifting = 0 <= step - 2 < BLOCKS
+            dividing = 0 <= step - 3
+            if step + 2 < BLOCKS:
+                x_raw[step + 2] = load_input(x, step + 2, "x")
+                y_raw[step + 2] = load_input(y, step + 2, "y")
+            if dividing:
+                powers, total = softmax_powers(windows[step - 3], shift[step - 3])
+            if projecting:
+                project_k(x_pixels, 0, k_grouped)
+                project_k(x_pixels, 1, k_grouped)
+                y_pixels = quantise_input(y_grouped, "y")
+            if step < K_BLOCKS:
+                quantise_k_block(k_grouped, step)
+            if preparing:
+                x_grouped = regroup_input(x_raw[step + 1], "x")
+                y_grouped = regroup_input(y_raw[step + 1], "y")
+            if projecting:
+                q_grouped = stage.tile([P, WIDTH, BLOCK_ROWS, PACK], BF16, name="q_grouped", align_bytes=64)
+                project_q(y_pixels, 0, q_grouped)
+                project_q(y_pixels, 1, q_grouped)
+            if dividing:
+                softmax_divide(step - 3, powers, total)
+                store_what_is_free(step - 3)
+            if correlating:
+                correlate(step - 1)
+                windows[step - 1] = read_back(step - 1)
+            if projecting:
+                project_q(y_pixels, 2, q_grouped)
+                project_q(y_pixels, 3, q_grouped)
+                this_x_pixels = x_pixels
+            if preparing:
+                x_pixels = quantise_input(x_grouped, "x")
+            if projecting:
+                k_grouped = new_k_block(step + 1)
+                project_k(this_x_pixels, 2, k_grouped)
+                project_k(this_x_pixels, 3, k_grouped)
+                nc.vector.quantize_mx(
+                    out=q_codes[:, step * BLOCK_PIXELS : (step + 1) * BLOCK_PIXELS].bitcast(FP8X4),
+                    scales=q_scales[:, step * BLOCK_PIXELS : (step + 1) * BLOCK_PIXELS],
+                    in_=q_grouped[:].rearrange("p j r t -> p (j r t)"),
+                )
+            if shifting:
+                shift[step - 2] = softmax_shift(windows[step - 2])

@@ -64,7 +64,7 @@ def tile_local_module_pa_t_kernel(tc, x, y, query_w, query_b, key_w, key_b, out)
     with ExitStack() as ctx:
         keep = ctx.enter_context(tc.tile_pool(name="keep", bufs=1))
         weight_stage = ctx.enter_context(tc.tile_pool(name="weight_stage", bufs=2))
-        raw_pool = ctx.enter_context(tc.tile_pool(name="raw", bufs=3))
+        raw_pool = ctx.enter_context(tc.tile_pool(name="raw", bufs=BLOCKS))
         stage = ctx.enter_context(tc.tile_pool(name="stage", bufs=2))
         k_stage = ctx.enter_context(tc.tile_pool(name="k_stage", bufs=3))
         small = ctx.enter_context(tc.tile_pool(name="small", bufs=2))
@@ -281,14 +281,16 @@ def tile_local_module_pa_t_kernel(tc, x, y, query_w, query_b, key_w, key_b, out)
         y_raw = {0: load_input(y, 0, "y")}
         key_bias = load_bias(key_b, "key_bias")
         query_bias = load_bias(query_b, "query_bias")
-        x_raw[1] = load_input(x, 1, "x")
-        y_raw[1] = load_input(y, 1, "y")
+        for block in range(1, BLOCKS):
+            x_raw[block] = load_input(x, block, "x")
+            y_raw[block] = load_input(y, block, "y")
 
         key_weight = quantise_weight(key_rows, "key_w")
         x_grouped = regroup_input(x_raw[0], "x")
         y_grouped = regroup_input(y_raw[0], "y")
-        x_pixels = quantise_input(x_grouped, "x")
+        next_x_pixels = quantise_input(x_grouped, "x")
         query_weight = quantise_weight(query_rows, "query_w")
+        next_y_pixels = quantise_input(y_grouped, "y")
 
         k_grouped = new_k_block(0)
         windows = {}
@@ -299,44 +301,42 @@ def tile_local_module_pa_t_kernel(tc, x, y, query_w, query_b, key_w, key_b, out)
             correlating = 0 <= step - 1 < BLOCKS
             shifting = 0 <= step - 2 < BLOCKS
             dividing = 0 <= step - 3
-            if step + 2 < BLOCKS:
-                x_raw[step + 2] = load_input(x, step + 2, "x")
-                y_raw[step + 2] = load_input(y, step + 2, "y")
+            x_pixels, y_pixels = next_x_pixels, next_y_pixels
             if dividing:
                 powers, total = softmax_powers(windows[step - 3], shift[step - 3])
             if projecting:
                 project_k(x_pixels, 0, k_grouped)
                 project_k(x_pixels, 1, k_grouped)
-                y_pixels = quantise_input(y_grouped, "y")
-            if step < K_BLOCKS:
-                quantise_k_block(k_grouped, step)
             if preparing:
                 x_grouped = regroup_input(x_raw[step + 1], "x")
                 y_grouped = regroup_input(y_raw[step + 1], "y")
             if projecting:
                 q_grouped = stage.tile([P, WIDTH, BLOCK_ROWS, PACK], BF16, name="q_grouped", align_bytes=64)
                 project_q(y_pixels, 0, q_grouped)
+            if step < K_BLOCKS:
+                quantise_k_block(k_grouped, step)
+            if projecting:
                 project_q(y_pixels, 1, q_grouped)
+                project_q(y_pixels, 2, q_grouped)
+                project_q(y_pixels, 3, q_grouped)
             if dividing:
                 softmax_divide(step - 3, powers, total)
                 store_what_is_free(step - 3)
             if correlating:
                 correlate(step - 1)
                 windows[step - 1] = read_back(step - 1)
-            if projecting:
-                project_q(y_pixels, 2, q_grouped)
-                project_q(y_pixels, 3, q_grouped)
-                this_x_pixels = x_pixels
             if preparing:
-                x_pixels = quantise_input(x_grouped, "x")
+                next_x_pixels = quantise_input(x_grouped, "x")
             if projecting:
                 k_grouped = new_k_block(step + 1)
-                project_k(this_x_pixels, 2, k_grouped)
-                project_k(this_x_pixels, 3, k_grouped)
+                project_k(x_pixels, 2, k_grouped)
+                project_k(x_pixels, 3, k_grouped)
                 nc.vector.quantize_mx(
                     out=q_codes[:, step * BLOCK_PIXELS : (step + 1) * BLOCK_PIXELS].bitcast(FP8X4),
                     scales=q_scales[:, step * BLOCK_PIXELS : (step + 1) * BLOCK_PIXELS],
                     in_=q_grouped[:].rearrange("p j r t -> p (j r t)"),
                 )
+            if preparing:
+                next_y_pixels = quantise_input(y_grouped, "y")
             if shifting:
                 shift[step - 2] = softmax_shift(windows[step - 2])

@@ -79,6 +79,10 @@ def tile_local_module_pa_t_kernel(tc, x, y, query_w, query_b, key_w, key_b, out)
         identity = keep.tile([P, P], BF16)
         make_identity(nc, identity[:])
 
+        warm = keep.tile([P, 1], F32)
+        nc.vector.memset(warm[:], 0.0)
+        nc.scalar.activation(out=warm[:], in_=warm[:], func=mybir.ActivationFunctionType.Exp)
+
         margin_words = K_MARGIN * BLOCK_ROWS
         code_blocks = k_codes[:].bitcast(I32).rearrange("p (b w) -> p b w", w=K_BLOCK_WORDS)
         scale_blocks = k_scales[:].bitcast(I32).rearrange("p (b w) -> p b w", w=K_BLOCK_WORDS // 4)
@@ -251,8 +255,12 @@ def tile_local_module_pa_t_kernel(tc, x, y, query_w, query_b, key_w, key_b, out)
         def softmax_divide(block, powers, total):
             inverse = small.tile([P, PAIRS], F32, name="inverse")
             nc.vector.reciprocal(out=inverse[:], in_=total[:])
-            for m in range(PAIRS):
-                nc.scalar.mul(out=result[:, block, m, :], in_=powers[:, m, :], mul=inverse[:, m : m + 1])
+            nc.gpsimd.tensor_tensor(
+                out=result[:, block],
+                in0=powers[:],
+                in1=inverse[:].unsqueeze(2).to_broadcast([P, PAIRS, CELLS]),
+                op=mybir.AluOpType.mult,
+            )
 
         def store(block):
             nc.sync.dma_start(
@@ -262,10 +270,13 @@ def tile_local_module_pa_t_kernel(tc, x, y, query_w, query_b, key_w, key_b, out)
                 in_=result[:, block],
             )
 
-        def store_what_is_free(block):
-            for done in range(block + 1):
-                if max(done, last_block_parked_on(done)) == block:
-                    store(done)
+        stored = set()
+
+        def store_what_is_free(divided, read):
+            for block in range(divided + 1):
+                if block not in stored and last_block_parked_on(block) <= read:
+                    store(block)
+                    stored.add(block)
 
         def project_k(pixels, pair, grouped):
             first = (2 * pair + REACH) % BLOCK_ROWS
@@ -321,10 +332,11 @@ def tile_local_module_pa_t_kernel(tc, x, y, query_w, query_b, key_w, key_b, out)
                 project_q(y_pixels, 3, q_grouped)
             if dividing:
                 softmax_divide(step - 3, powers, total)
-                store_what_is_free(step - 3)
+                store_what_is_free(divided=step - 3, read=min(step - 2, BLOCKS - 1))
             if correlating:
                 correlate(step - 1)
                 windows[step - 1] = read_back(step - 1)
+                store_what_is_free(divided=step - 3, read=step - 1)
             if preparing:
                 next_x_pixels = quantise_input(x_grouped, "x")
             if projecting:

@@ -46,6 +46,9 @@ OUT_FLOATS = HEIGHT * WIDTH * CELLS
 OUT_BLOCK = BLOCK_PIXELS * CELLS
 PARK_START = OUT_FLOATS - PARK_SLOTS * PARK_BLOCK
 
+SHIFT_AFTER = 3
+DIVIDE_AFTER = SHIFT_AFTER + 1
+
 FLOPS = 2 * 2 * CHANNELS * CHANNELS * HEIGHT * WIDTH + 2 * CHANNELS * CELLS * HEIGHT * WIDTH
 
 
@@ -67,6 +70,7 @@ def tile_local_module_pa_t_kernel(tc, x, y, query_w, query_b, key_w, key_b, out)
         raw_pool = ctx.enter_context(tc.tile_pool(name="raw", bufs=BLOCKS))
         stage = ctx.enter_context(tc.tile_pool(name="stage", bufs=2))
         k_stage = ctx.enter_context(tc.tile_pool(name="k_stage", bufs=3))
+        late = ctx.enter_context(tc.tile_pool(name="late", bufs=DIVIDE_AFTER))
         small = ctx.enter_context(tc.tile_pool(name="small", bufs=2))
         project_psum = ctx.enter_context(tc.psum_pool(name="project_psum", bufs=4))
         corr_psum = ctx.enter_context(tc.psum_pool(name="corr_psum", bufs=4))
@@ -76,7 +80,7 @@ def tile_local_module_pa_t_kernel(tc, x, y, query_w, query_b, key_w, key_b, out)
         k_codes = keep.tile([P, K_BLOCKS * K_BLOCK_WORDS], U32, align_bytes=64)
         k_scales = keep.tile([P, K_BLOCKS * K_BLOCK_WORDS], U8, align_bytes=64)
         result = keep.tile([P, BLOCKS, PAIRS, CELLS], F32)
-        identity = keep.tile([P, P], BF16)
+        identity = keep.tile([P, P], F32)
         make_identity(nc, identity[:])
 
         warm = keep.tile([P, 1], F32)
@@ -96,15 +100,23 @@ def tile_local_module_pa_t_kernel(tc, x, y, query_w, query_b, key_w, key_b, out)
             nc.sync.dma_start(out=rows[:], in_=w.rearrange("(p m) c -> p m c", m=PACK))
             return rows
 
-        def quantise_weight(rows, name):
+        def regroup_weight(rows):
             grouped = weight_stage.tile([P, CHANNELS, PACK], BF16, name="w_grouped", align_bytes=64)
-            for m in range(PACK):
-                flipped = corr_psum.tile([P, PACK, P], BF16, name="flipped", tag="corr_bank")
-                for j in range(PACK):
-                    nc.tensor.transpose(flipped[:, j, :], rows[:, m, j * P : (j + 1) * P], identity[:])
+            for half in range(2):
+                flipped = corr_psum.tile([P, 2, 2, P], F32, name="flipped", tag="corr_bank")
+                for m in range(2):
+                    pairs = rows[:, 2 * half + m, :].bitcast(F32)
+                    for u in range(2):
+                        nc.tensor.transpose(flipped[:, m, u, :], pairs[:, u * P : (u + 1) * P], identity[:])
                 nc.vector.tensor_copy(
-                    out=grouped[:, m * P : (m + 1) * P, :], in_=flipped[:].rearrange("p j o -> p o j")
+                    out=grouped[:, 2 * half * P : (2 * half + 2) * P, :]
+                    .bitcast(F32)
+                    .rearrange("p (m o) u -> p m o u", m=2),
+                    in_=flipped[:].rearrange("p m u o -> p m o u"),
                 )
+            return grouped
+
+        def quantise_weight(grouped, name):
             codes = keep.tile([P, CHANNELS], U32, name=name + "_codes", align_bytes=64)
             scales = keep.tile([P, CHANNELS], U8, name=name + "_scales", align_bytes=64)
             nc.vector.quantize_mx(
@@ -114,13 +126,17 @@ def tile_local_module_pa_t_kernel(tc, x, y, query_w, query_b, key_w, key_b, out)
 
         def load_bias(b, name):
             bias = keep.tile([P, PACK], BF16, name=name)
-            nc.sync.dma_start(out=bias[:], in_=b.rearrange("(p t) -> p t", t=PACK))
+            nc.scalar.dma_start(out=bias[:], in_=b.rearrange("(p t) -> p t", t=PACK))
             return bias
 
         def load_input(image, block, name):
-            planes = image.rearrange("b (j p) h w -> p (b j) (h w)", p=P)
+            halves = image.rearrange("b (u p e) h w -> u p (b e) (h w)", u=2, e=2)
             raw = raw_pool.tile([P, PACK, BLOCK_PIXELS], BF16, name=name + "_raw")
-            nc.sync.dma_start(out=raw[:], in_=planes[:, :, block * BLOCK_PIXELS : (block + 1) * BLOCK_PIXELS])
+            for u in range(2):
+                nc.sync.dma_start(
+                    out=raw[:, 2 * u : 2 * u + 2, :],
+                    in_=halves[u, :, :, block * BLOCK_PIXELS : (block + 1) * BLOCK_PIXELS],
+                )
             return raw
 
         def regroup_input(raw, name):
@@ -198,11 +214,12 @@ def tile_local_module_pa_t_kernel(tc, x, y, query_w, query_b, key_w, key_b, out)
                         start=True,
                         stop=True,
                     )
-                nc.scalar.copy(
+                nc.scalar.mul(
                     out=products[:, patch, :].rearrange("p (h r c) -> p h r c", h=2, r=BLOCK_ROWS),
                     in_=bank[:].rearrange("p h (c r) -> p h r c", r=BLOCK_ROWS)[
                         :, :, :, STREAM_SKIP : STREAM_SKIP + WINDOW_COLS
                     ],
+                    mul=1.0 / CHANNELS,
                 )
             for r in range(BLOCK_ROWS):
                 row_base = park_base(block) + r * PARK_ROW
@@ -216,7 +233,7 @@ def tile_local_module_pa_t_kernel(tc, x, y, query_w, query_b, key_w, key_b, out)
                 )
 
         def read_back(block):
-            windows = stage.tile([P, PAIRS, PARK_RUN], F32, name="windows")
+            windows = late.tile([P, PAIRS, PARK_RUN], F32, name="windows")
             base = park_base(block)
             nc.sync.dma_start(
                 out=windows[:, :, 0:PARK_READ],
@@ -230,12 +247,14 @@ def tile_local_module_pa_t_kernel(tc, x, y, query_w, query_b, key_w, key_b, out)
             return windows[:].rearrange("p m (d c) -> p m d c", c=WINDOW_COLS)[:, :, :, 0:SHIFTS]
 
         def softmax_shift(windows):
-            top = small.tile([P, PAIRS], F32, name="top")
+            shift = late.tile([P, PAIRS], F32, name="shift")
             nc.vector.tensor_reduce(
-                out=top[:], in_=window_cells(windows), axis=mybir.AxisListType.XY, op=mybir.AluOpType.max
+                out=shift[:],
+                in_=window_cells(windows),
+                axis=mybir.AxisListType.XY,
+                op=mybir.AluOpType.max,
+                negate=True,
             )
-            shift = small.tile([P, PAIRS], F32, name="shift")
-            nc.vector.tensor_scalar_mul(out=shift[:], in0=top[:], scalar1=-1.0 / CHANNELS)
             return shift
 
         def softmax_powers(windows, shift):
@@ -247,7 +266,6 @@ def tile_local_module_pa_t_kernel(tc, x, y, query_w, query_b, key_w, key_b, out)
                     in_=window_cells(windows)[:, m],
                     func=mybir.ActivationFunctionType.Exp,
                     bias=shift[:, m : m + 1],
-                    scale=1.0 / CHANNELS,
                     accum_out=total[:, m : m + 1],
                 )
             return powers, total
@@ -255,12 +273,8 @@ def tile_local_module_pa_t_kernel(tc, x, y, query_w, query_b, key_w, key_b, out)
         def softmax_divide(block, powers, total):
             inverse = small.tile([P, PAIRS], F32, name="inverse")
             nc.vector.reciprocal(out=inverse[:], in_=total[:])
-            nc.gpsimd.tensor_tensor(
-                out=result[:, block],
-                in0=powers[:],
-                in1=inverse[:].unsqueeze(2).to_broadcast([P, PAIRS, CELLS]),
-                op=mybir.AluOpType.mult,
-            )
+            for m in range(PAIRS):
+                nc.scalar.mul(out=result[:, block, m, :], in_=powers[:, m, :], mul=inverse[:, m : m + 1])
 
         def store(block):
             nc.sync.dma_start(
@@ -286,38 +300,38 @@ def tile_local_module_pa_t_kernel(tc, x, y, query_w, query_b, key_w, key_b, out)
             project(pixels, pair, query_weight, query_bias, grouped[:, :, 2 * pair : 2 * pair + 2, :])
 
         ctx.enter_context(tc.manual_schedule())
+        key_bias = load_bias(key_b, "key_bias")
+        query_bias = load_bias(query_b, "query_bias")
         key_rows = load_weight(key_w)
         x_raw = {0: load_input(x, 0, "x")}
         query_rows = load_weight(query_w)
         y_raw = {0: load_input(y, 0, "y")}
-        key_bias = load_bias(key_b, "key_bias")
-        query_bias = load_bias(query_b, "query_bias")
         for block in range(1, BLOCKS):
             x_raw[block] = load_input(x, block, "x")
             y_raw[block] = load_input(y, block, "y")
 
-        key_weight = quantise_weight(key_rows, "key_w")
+        key_weight = quantise_weight(regroup_weight(key_rows), "key_w")
         x_grouped = regroup_input(x_raw[0], "x")
         y_grouped = regroup_input(y_raw[0], "y")
+        query_grouped = regroup_weight(query_rows)
         next_x_pixels = quantise_input(x_grouped, "x")
-        query_weight = quantise_weight(query_rows, "query_w")
+        query_weight = quantise_weight(query_grouped, "query_w")
+        next_k_grouped = new_k_block(0)
+        project_k(next_x_pixels, 0, next_k_grouped)
         next_y_pixels = quantise_input(y_grouped, "y")
+        project_k(next_x_pixels, 1, next_k_grouped)
 
-        k_grouped = new_k_block(0)
         windows = {}
         shift = {}
-        for step in range(BLOCKS + 3):
+        for step in range(BLOCKS + DIVIDE_AFTER):
             projecting = step < BLOCKS
             preparing = step + 1 < BLOCKS
             correlating = 0 <= step - 1 < BLOCKS
-            shifting = 0 <= step - 2 < BLOCKS
-            dividing = 0 <= step - 3
-            x_pixels, y_pixels = next_x_pixels, next_y_pixels
+            shifting = 0 <= step - SHIFT_AFTER < BLOCKS
+            dividing = 0 <= step - DIVIDE_AFTER
+            x_pixels, y_pixels, k_grouped = next_x_pixels, next_y_pixels, next_k_grouped
             if dividing:
-                powers, total = softmax_powers(windows[step - 3], shift[step - 3])
-            if projecting:
-                project_k(x_pixels, 0, k_grouped)
-                project_k(x_pixels, 1, k_grouped)
+                powers, total = softmax_powers(windows[step - DIVIDE_AFTER], shift[step - DIVIDE_AFTER])
             if preparing:
                 x_grouped = regroup_input(x_raw[step + 1], "x")
                 y_grouped = regroup_input(y_raw[step + 1], "y")
@@ -331,24 +345,25 @@ def tile_local_module_pa_t_kernel(tc, x, y, query_w, query_b, key_w, key_b, out)
                 project_q(y_pixels, 2, q_grouped)
                 project_q(y_pixels, 3, q_grouped)
             if dividing:
-                softmax_divide(step - 3, powers, total)
-                store_what_is_free(divided=step - 3, read=min(step - 2, BLOCKS - 1))
+                softmax_divide(step - DIVIDE_AFTER, powers, total)
             if correlating:
                 correlate(step - 1)
                 windows[step - 1] = read_back(step - 1)
-                store_what_is_free(divided=step - 3, read=step - 1)
+            store_what_is_free(divided=step - DIVIDE_AFTER, read=min(step - 2, BLOCKS - 1))
             if preparing:
                 next_x_pixels = quantise_input(x_grouped, "x")
             if projecting:
-                k_grouped = new_k_block(step + 1)
-                project_k(x_pixels, 2, k_grouped)
-                project_k(x_pixels, 3, k_grouped)
+                next_k_grouped = new_k_block(step + 1)
+                project_k(x_pixels, 2, next_k_grouped)
+                project_k(x_pixels, 3, next_k_grouped)
                 nc.vector.quantize_mx(
                     out=q_codes[:, step * BLOCK_PIXELS : (step + 1) * BLOCK_PIXELS].bitcast(FP8X4),
                     scales=q_scales[:, step * BLOCK_PIXELS : (step + 1) * BLOCK_PIXELS],
                     in_=q_grouped[:].rearrange("p j r t -> p (j r t)"),
                 )
             if preparing:
+                project_k(next_x_pixels, 0, next_k_grouped)
                 next_y_pixels = quantise_input(y_grouped, "y")
+                project_k(next_x_pixels, 1, next_k_grouped)
             if shifting:
-                shift[step - 2] = softmax_shift(windows[step - 2])
+                shift[step - SHIFT_AFTER] = softmax_shift(windows[step - SHIFT_AFTER])

from contextlib import ExitStack

import concourse.mybir as mybir
from concourse.masks import make_identity

F32 = mybir.dt.float32
BF16 = mybir.dt.bfloat16
U32 = mybir.dt.uint32
U8 = mybir.dt.uint8
I32 = mybir.dt.int32
FP8X4 = mybir.dt.float8_e4m3fn_x4

P = 128
PACK = 4
CHANNELS = P * PACK
HEIGHT = 64
WIDTH = 64
REACH = 4
SHIFTS = 2 * REACH + 1
CELLS = SHIFTS * SHIFTS

BLOCK_ROWS = 8
BLOCKS = HEIGHT // BLOCK_ROWS
BLOCK_PIXELS = BLOCK_ROWS * WIDTH
PAIR_PIXELS = 2 * WIDTH
PAIRS = BLOCK_ROWS // 2

PATCH_COLS = P // BLOCK_ROWS
PATCHES = WIDTH // PATCH_COLS
WINDOW_ROWS = BLOCK_ROWS + 2 * REACH
WINDOW_COLS = PATCH_COLS + 2 * REACH
K_BLOCKS = BLOCKS + 1
K_MARGIN = 8
K_COLS = WIDTH + 2 * K_MARGIN
K_BLOCK_WORDS = K_COLS * BLOCK_ROWS
STREAM_COLS = 32
STREAM_SKIP = K_MARGIN - REACH

PARK_RUN = SHIFTS * WINDOW_COLS
PARK_STEP = PARK_RUN + 1
PARK_READ = (SHIFTS - 1) * WINDOW_COLS + SHIFTS
PARK_ROW = WIDTH * PARK_STEP
PARK_BLOCK = BLOCK_ROWS * PARK_ROW
PARK_SLOTS = 2
OUT_FLOATS = HEIGHT * WIDTH * CELLS
OUT_BLOCK = BLOCK_PIXELS * CELLS
PARK_START = OUT_FLOATS - PARK_SLOTS * PARK_BLOCK

SHIFT_AFTER = 3
DIVIDE_AFTER = SHIFT_AFTER + 1

FLOPS = 2 * 2 * CHANNELS * CHANNELS * HEIGHT * WIDTH + 2 * CHANNELS * CELLS * HEIGHT * WIDTH


def park_base(block):
    return PARK_START + (block % PARK_SLOTS) * PARK_BLOCK


def last_block_parked_on(block):
    first, end = block * OUT_BLOCK, (block + 1) * OUT_BLOCK
    users = [b for b in range(BLOCKS) if park_base(b) < end and first < park_base(b) + PARK_BLOCK]
    return max(users) if users else -1


def tile_local_module_pa_t_kernel(tc, x, y, query_w, query_b, key_w, key_b, out):
    nc = tc.nc
    with ExitStack() as ctx:
        keep = ctx.enter_context(tc.tile_pool(name="keep", bufs=1))
        weight_stage = ctx.enter_context(tc.tile_pool(name="weight_stage", bufs=2))
        raw_pool = ctx.enter_context(tc.tile_pool(name="raw", bufs=BLOCKS))
        stage = ctx.enter_context(tc.tile_pool(name="stage", bufs=2))
        k_stage = ctx.enter_context(tc.tile_pool(name="k_stage", bufs=3))
        late = ctx.enter_context(tc.tile_pool(name="late", bufs=DIVIDE_AFTER))
        small = ctx.enter_context(tc.tile_pool(name="small", bufs=2))
        project_psum = ctx.enter_context(tc.psum_pool(name="project_psum", bufs=4))
        corr_psum = ctx.enter_context(tc.psum_pool(name="corr_psum", bufs=4))

        q_codes = keep.tile([P, BLOCKS * BLOCK_PIXELS], U32, align_bytes=64)
        q_scales = keep.tile([P, BLOCKS * BLOCK_PIXELS], U8, align_bytes=64)
        k_codes = keep.tile([P, K_BLOCKS * K_BLOCK_WORDS], U32, align_bytes=64)
        k_scales = keep.tile([P, K_BLOCKS * K_BLOCK_WORDS], U8, align_bytes=64)
        result = keep.tile([P, BLOCKS, PAIRS, CELLS], F32)
        identity = keep.tile([P, P], F32)
        make_identity(nc, identity[:])

        warm = keep.tile([P, 1], F32)
        nc.vector.memset(warm[:], 0.0)
        nc.scalar.activation(out=warm[:], in_=warm[:], func=mybir.ActivationFunctionType.Exp)

        margin_words = K_MARGIN * BLOCK_ROWS
        code_blocks = k_codes[:].bitcast(I32).rearrange("p (b w) -> p b w", w=K_BLOCK_WORDS)
        scale_blocks = k_scales[:].bitcast(I32).rearrange("p (b w) -> p b w", w=K_BLOCK_WORDS // 4)
        nc.vector.memset(code_blocks[:, :, 0:margin_words], 0)
        nc.vector.memset(code_blocks[:, :, K_BLOCK_WORDS - margin_words :], 0)
        nc.vector.memset(scale_blocks[:, :, 0 : margin_words // 4], 0)
        nc.vector.memset(scale_blocks[:, :, (K_BLOCK_WORDS - margin_words) // 4 :], 0)

        def load_weight(w):
            rows = weight_stage.tile([P, PACK, CHANNELS], BF16, name="w_rows")
            nc.sync.dma_start(out=rows[:], in_=w.rearrange("(p m) c -> p m c", m=PACK))
            return rows

        def regroup_weight(rows):
            grouped = weight_stage.tile([P, CHANNELS, PACK], BF16, name="w_grouped", align_bytes=64)
            for half in range(2):
                flipped = corr_psum.tile([P, 2, 2, P], F32, name="flipped", tag="corr_bank")
                for m in range(2):
                    pairs = rows[:, 2 * half + m, :].bitcast(F32)
                    for u in range(2):
                        nc.tensor.transpose(flipped[:, m, u, :], pairs[:, u * P : (u + 1) * P], identity[:])
                nc.vector.tensor_copy(
                    out=grouped[:, 2 * half * P : (2 * half + 2) * P, :]
                    .bitcast(F32)
                    .rearrange("p (m o) u -> p m o u", m=2),
                    in_=flipped[:].rearrange("p m u o -> p m o u"),
                )
            return grouped

        def quantise_weight(grouped, name):
            codes = keep.tile([P, CHANNELS], U32, name=name + "_codes", align_bytes=64)
            scales = keep.tile([P, CHANNELS], U8, name=name + "_scales", align_bytes=64)
            nc.vector.quantize_mx(
                out=codes[:].bitcast(FP8X4), scales=scales[:], in_=grouped[:].rearrange("p o j -> p (o j)")
            )
            return codes, scales

        def load_bias(b, name):
            bias = keep.tile([P, PACK], BF16, name=name)
            nc.scalar.dma_start(out=bias[:], in_=b.rearrange("(p t) -> p t", t=PACK))
            return bias

        def load_input(image, block, name):
            halves = image.rearrange("b (u p e) h w -> u p (b e) (h w)", u=2, e=2)
            raw = raw_pool.tile([P, PACK, BLOCK_PIXELS], BF16, name=name + "_raw")
            for u in range(2):
                nc.sync.dma_start(
                    out=raw[:, 2 * u : 2 * u + 2, :],
                    in_=halves[u, :, :, block * BLOCK_PIXELS : (block + 1) * BLOCK_PIXELS],
                )
            return raw

        def regroup_input(raw, name):
            grouped = stage.tile([P, BLOCK_PIXELS, PACK], BF16, name=name + "_grouped", align_bytes=64)
            nc.scalar.copy(
                out=grouped[:].rearrange("p (c i) j -> p c j i", i=4),
                in_=raw[:].rearrange("p j (c i) -> p c j i", i=4),
            )
            return grouped

        def quantise_input(grouped, name):
            codes = stage.tile([P, BLOCK_PIXELS], U32, name=name + "_codes", align_bytes=64)
            scales = stage.tile([P, BLOCK_PIXELS], U8, name=name + "_scales", align_bytes=64)
            nc.vector.quantize_mx(
                out=codes[:].bitcast(FP8X4), scales=scales[:], in_=grouped[:].rearrange("p w j -> p (w j)")
            )
            return codes, scales

        def project(pixels, pair, weight, bias, target):
            codes, scales = pixels
            w_codes, w_scales = weight
            cols = slice(pair * PAIR_PIXELS, (pair + 1) * PAIR_PIXELS)
            bank = project_psum.tile([P, PACK, PAIR_PIXELS], F32, name="bank")
            for t in range(PACK):
                channels = slice(t * P, (t + 1) * P)
                nc.tensor.matmul_mx(
                    out=bank[:, t, :],
                    lhsT=w_codes[:, channels].bitcast(FP8X4),
                    lhsT_scale=w_scales[:, channels],
                    rhs=codes[:, cols].bitcast(FP8X4),
                    rhs_scale=scales[:, cols],
                    start=True,
                    stop=True,
                )
            nc.vector.tensor_tensor(
                out=target,
                in0=bank[:].rearrange("p t (i j) -> p j i t", i=2),
                in1=bias[:].unsqueeze(1).unsqueeze(1).to_broadcast([P, WIDTH, 2, PACK]),
                op=mybir.AluOpType.add,
            )

        def new_k_block(k_block):
            grouped = k_stage.tile([P, WIDTH, BLOCK_ROWS, PACK], BF16, name="k_grouped", align_bytes=64)
            if k_block == 0:
                nc.vector.memset(grouped[:, :, 0:REACH, :], 0.0)
            if k_block == K_BLOCKS - 1:
                nc.vector.memset(grouped[:, :, REACH:, :], 0.0)
            return grouped

        def quantise_k_block(grouped, k_block):
            first = k_block * K_BLOCK_WORDS + margin_words
            nc.vector.quantize_mx(
                out=k_codes[:, first : first + BLOCK_PIXELS].bitcast(FP8X4),
                scales=k_scales[:, first : first + BLOCK_PIXELS],
                in_=grouped[:].rearrange("p j r t -> p (j r t)"),
            )

        out_flat = out.rearrange("b h w d -> (b h w d)")
        out_pixels = out.rearrange("b h w d -> (b h w) d")

        def correlate(block):
            products = stage.tile([P, PATCHES, WINDOW_ROWS * WINDOW_COLS], F32, name="products")
            for patch in range(PATCHES):
                q_cols = slice(block * BLOCK_PIXELS + patch * P, block * BLOCK_PIXELS + (patch + 1) * P)
                bank = corr_psum.tile([P, 2, STREAM_COLS * BLOCK_ROWS], F32, name="corr_bank")
                for half in range(2):
                    first = (block + half) * K_BLOCK_WORDS + patch * PATCH_COLS * BLOCK_ROWS
                    k_cols = slice(first, first + STREAM_COLS * BLOCK_ROWS)
                    nc.tensor.matmul_mx(
                        out=bank[:, half, :],
                        lhsT=q_codes[:, q_cols].bitcast(FP8X4),
                        lhsT_scale=q_scales[:, q_cols],
                        rhs=k_codes[:, k_cols].bitcast(FP8X4),
                        rhs_scale=k_scales[:, k_cols],
                        start=True,
                        stop=True,
                    )
                nc.scalar.mul(
                    out=products[:, patch, :].rearrange("p (h r c) -> p h r c", h=2, r=BLOCK_ROWS),
                    in_=bank[:].rearrange("p h (c r) -> p h r c", r=BLOCK_ROWS)[
                        :, :, :, STREAM_SKIP : STREAM_SKIP + WINDOW_COLS
                    ],
                    mul=1.0 / CHANNELS,
                )
            for r in range(BLOCK_ROWS):
                row_base = park_base(block) + r * PARK_ROW
                parked = (
                    out_flat[row_base : row_base + PARK_ROW]
                    .rearrange("(a s) -> a s", s=PATCH_COLS * PARK_STEP)[:, 0 : PATCH_COLS * PARK_RUN]
                    .rearrange("a (c s) -> c a s", s=PARK_RUN)
                )
                nc.sync.dma_start(
                    out=parked, in_=products[r:P:BLOCK_ROWS, :, r * WINDOW_COLS : r * WINDOW_COLS + PARK_RUN]
                )

        def read_back(block):
            windows = late.tile([P, PAIRS, PARK_RUN], F32, name="windows")
            base = park_base(block)
            nc.sync.dma_start(
                out=windows[:, :, 0:PARK_READ],
                in_=out_flat[base : base + PARK_BLOCK].rearrange("(m p s) -> p m s", p=P, s=PARK_STEP)[
                    :, :, 0:PARK_READ
                ],
            )
            return windows

        def window_cells(windows):
            return windows[:].rearrange("p m (d c) -> p m d c", c=WINDOW_COLS)[:, :, :, 0:SHIFTS]

        def softmax_shift(windows):
            shift = late.tile([P, PAIRS], F32, name="shift")
            nc.vector.tensor_reduce(
                out=shift[:],
                in_=window_cells(windows),
                axis=mybir.AxisListType.XY,
                op=mybir.AluOpType.max,
                negate=True,
            )
            return shift

        def softmax_powers(windows, shift):
            powers = stage.tile([P, PAIRS, CELLS], F32, name="powers")
            total = small.tile([P, PAIRS], F32, name="total")
            for m in range(PAIRS):
                nc.scalar.activation(
                    out=powers[:, m, :].rearrange("p (d c) -> p d c", c=SHIFTS),
                    in_=window_cells(windows)[:, m],
                    func=mybir.ActivationFunctionType.Exp,
                    bias=shift[:, m : m + 1],
                    accum_out=total[:, m : m + 1],
                )
            return powers, total

        def softmax_divide(block, powers, total):
            inverse = small.tile([P, PAIRS], F32, name="inverse")
            nc.vector.reciprocal(out=inverse[:], in_=total[:])
            for m in range(PAIRS):
                nc.scalar.mul(out=result[:, block, m, :], in_=powers[:, m, :], mul=inverse[:, m : m + 1])

        def store(block):
            nc.sync.dma_start(
                out=out_pixels[block * BLOCK_PIXELS : (block + 1) * BLOCK_PIXELS, :].rearrange(
                    "(m p) d -> p m d", p=P
                ),
                in_=result[:, block],
            )

        stored = set()

        def store_what_is_free(divided, read):
            for block in range(divided + 1):
                if block not in stored and last_block_parked_on(block) <= read:
                    store(block)
                    stored.add(block)

        def project_k(pixels, pair, grouped):
            first = (2 * pair + REACH) % BLOCK_ROWS
            project(pixels, pair, key_weight, key_bias, grouped[:, :, first : first + 2, :])

        def project_q(pixels, pair, grouped):
            project(pixels, pair, query_weight, query_bias, grouped[:, :, 2 * pair : 2 * pair + 2, :])

        ctx.enter_context(tc.manual_schedule())
        key_bias = load_bias(key_b, "key_bias")
        query_bias = load_bias(query_b, "query_bias")
        key_rows = load_weight(key_w)
        x_raw = {0: load_input(x, 0, "x")}
        query_rows = load_weight(query_w)
        y_raw = {0: load_input(y, 0, "y")}
        for block in range(1, BLOCKS):
            x_raw[block] = load_input(x, block, "x")
            y_raw[block] = load_input(y, block, "y")

        key_weight = quantise_weight(regroup_weight(key_rows), "key_w")
        x_grouped = regroup_input(x_raw[0], "x")
        y_grouped = regroup_input(y_raw[0], "y")
        query_grouped = regroup_weight(query_rows)
        next_x_pixels = quantise_input(x_grouped, "x")
        query_weight = quantise_weight(query_grouped, "query_w")
        next_k_grouped = new_k_block(0)
        project_k(next_x_pixels, 0, next_k_grouped)
        next_y_pixels = quantise_input(y_grouped, "y")
        project_k(next_x_pixels, 1, next_k_grouped)

        windows = {}
        shift = {}
        for step in range(BLOCKS + DIVIDE_AFTER):
            projecting = step < BLOCKS
            preparing = step + 1 < BLOCKS
            correlating = 0 <= step - 1 < BLOCKS
            shifting = 0 <= step - SHIFT_AFTER < BLOCKS
            dividing = 0 <= step - DIVIDE_AFTER
            x_pixels, y_pixels, k_grouped = next_x_pixels, next_y_pixels, next_k_grouped
            if dividing:
                powers, total = softmax_powers(windows[step - DIVIDE_AFTER], shift[step - DIVIDE_AFTER])
            if preparing:
                x_grouped = regroup_input(x_raw[step + 1], "x")
                y_grouped = regroup_input(y_raw[step + 1], "y")
            if projecting:
                q_grouped = stage.tile([P, WIDTH, BLOCK_ROWS, PACK], BF16, name="q_grouped", align_bytes=64)
                project_q(y_pixels, 0, q_grouped)
            if step < K_BLOCKS:
                quantise_k_block(k_grouped, step)
            if projecting:
                project_q(y_pixels, 1, q_grouped)
                project_q(y_pixels, 2, q_grouped)
                project_q(y_pixels, 3, q_grouped)
            if dividing:
                softmax_divide(step - DIVIDE_AFTER, powers, total)
            if correlating:
                correlate(step - 1)
                windows[step - 1] = read_back(step - 1)
            store_what_is_free(divided=step - DIVIDE_AFTER, read=min(step - 2, BLOCKS - 1))
            if preparing:
                next_x_pixels = quantise_input(x_grouped, "x")
            if projecting:
                next_k_grouped = new_k_block(step + 1)
                project_k(x_pixels, 2, next_k_grouped)
                project_k(x_pixels, 3, next_k_grouped)
                nc.vector.quantize_mx(
                    out=q_codes[:, step * BLOCK_PIXELS : (step + 1) * BLOCK_PIXELS].bitcast(FP8X4),
                    scales=q_scales[:, step * BLOCK_PIXELS : (step + 1) * BLOCK_PIXELS],
                    in_=q_grouped[:].rearrange("p j r t -> p (j r t)"),
                )
            if preparing:
                project_k(next_x_pixels, 0, next_k_grouped)
                next_y_pixels = quantise_input(y_grouped, "y")
                project_k(next_x_pixels, 1, next_k_grouped)
            if shifting:
                shift[step - SHIFT_AFTER] = softmax_shift(windows[step - SHIFT_AFTER])
